import numpy as np
import ml_dtypes


def mxq(x, axis, fmt="e4m3"):
    dtype, down = {"e4m3": (ml_dtypes.float8_e4m3fn, 7), "e5m2": (ml_dtypes.float8_e5m2, 14)}[fmt]
    v = np.moveaxis(np.asarray(x, np.float32).astype(ml_dtypes.bfloat16).astype(np.float64), axis, -1)
    blocks = v.reshape(v.shape[:-1] + (-1, 32))
    amax = np.abs(blocks).max(-1, keepdims=True)
    byte = np.maximum(np.where(amax > 0, np.frexp(amax)[1] - 1 + 127, 0) - down, 1)
    scale = np.exp2(byte - 127.0)
    codes = (blocks / scale).astype(np.float32).astype(dtype).astype(np.float64)
    return np.moveaxis((codes * scale).reshape(v.shape), -1, axis)


WIDE = False


def mx_kscale(k):
    if not WIDE:
        return np.ones(k)
    levels = np.array([10, -10, 5, -5, 0])
    if k % 512:
        return np.exp2(np.random.permutation(np.resize(levels, k // 32))).repeat(32)
    a = np.empty((k // 512, 16))
    for p in range(k // 512):
        a[p, :8] = np.random.permutation(np.resize(levels, 8))
        for g in range(8):
            far = levels[np.abs(levels - a[p, g]) >= 10]
            a[p, g + 8] = far[np.random.randint(len(far))]
    return np.exp2(a.ravel()).repeat(32)


BF16 = ml_dtypes.bfloat16


def bf(x):
    return np.asarray(x, np.float32).astype(BF16)


def f64(x):
    return np.asarray(x).astype(np.float64)


B, T, I, H = 128, 64, 1024, 128


def sigmoid(v):
    return 1.0 / (1.0 + np.exp(-v))


def setup_inputs():
    s = mx_kscale(I)
    d = {"inputs": bf(np.random.standard_normal((B, T, I)) * s),
         "h0": bf(np.random.standard_normal((1, B, H))),
         "c0": bf(np.random.standard_normal((1, B, H)))}
    for ni, nh in (("ii", "hi"), ("if_", "hf"), ("io", "ho"), ("ig", "hg")):
        d["w_" + ni] = bf(np.random.standard_normal((H, I)) / np.sqrt(I) / s[None, :])
        d["b_" + ni] = bf(np.random.standard_normal((H, 1)) * 0.3)
        d["w_" + nh] = bf(np.random.standard_normal((H, H)) * 0.7 / np.sqrt(H))
        d["b_" + nh] = bf(np.random.standard_normal((H, 1)) * 0.3)
    return d


def reference(inputs, h0, c0, w_ii, b_ii, w_hi, b_hi, w_if_, b_if_, w_hf, b_hf, w_io, b_io, w_ho, b_ho, w_ig, b_ig, w_hg, b_hg):
    xq = mxq(f64(inputs), 2, "e4m3")
    h0s = f64(h0)[0]
    c0s = f64(c0)[0]
    zi = (xq @ mxq(f64(w_ii), 1, "e4m3").T) + (h0s @ f64(w_hi).T)[:, None, :] + f64(b_ii)[:, 0] + f64(b_hi)[:, 0]
    zf = (xq @ mxq(f64(w_if_), 1, "e4m3").T) + (h0s @ f64(w_hf).T)[:, None, :] + f64(b_if_)[:, 0] + f64(b_hf)[:, 0]
    zg = (xq @ mxq(f64(w_ig), 1, "e4m3").T) + (h0s @ f64(w_hg).T)[:, None, :] + f64(b_ig)[:, 0] + f64(b_hg)[:, 0]
    zo = (xq @ mxq(f64(w_io), 1, "e4m3").T) + (h0s @ f64(w_ho).T)[:, None, :] + f64(b_io)[:, 0] + f64(b_ho)[:, 0]
    i = sigmoid(zi)
    f = sigmoid(zf)
    g = np.tanh(zg)
    o = sigmoid(zo)
    c_next = f * c0s[:, None, :] + i * g
    h_next = o * np.tanh(c_next)
    hidden_seq = np.transpose(h_next, (1, 0, 2))
    h_last = hidden_seq[-1][None]
    c_last = c_next[:, -1][None]
    return hidden_seq, h_last, c_last

@@ -1,0 +1,267 @@
+from contextlib import ExitStack
+
+import concourse.mybir as mybir
+from concourse.masks import make_identity
+
+FP8X4 = mybir.dt.float8_e4m3fn_x4
+BF16 = mybir.dt.bfloat16
+F32 = mybir.dt.float32
+I32 = mybir.dt.int32
+U32 = mybir.dt.uint32
+U8 = mybir.dt.uint8
+ACT = mybir.ActivationFunctionType
+ALU = mybir.AluOpType
+
+B, T, I, H = 128, 64, 1024, 128
+P = 128
+G4 = 4 * H
+TC = 4
+NCH = T // TC
+XBUFS = 8
+FLOPS = 2 * B * T * I * G4 + 2 * B * H * G4
+
+
+def tile_naivelstm_pa_t_kernel(
+    tc, inputs, h0, c0, w_ii, b_ii, w_hi, b_hi, w_if_, b_if_, w_hf, b_hf,
+    w_io, b_io, w_ho, b_ho, w_ig, b_ig, w_hg, b_hg, out_0, out_1, out_2,
+):
+    nc = tc.nc
+    w_in = [w_ii, w_if_, w_io, w_ig]
+    w_hid = [w_hi, w_hf, w_ho, w_hg]
+    b_in = [b_ii, b_if_, b_io, b_ig]
+    b_hid = [b_hi, b_hf, b_ho, b_hg]
+
+    with ExitStack() as ctx:
+        consts = ctx.enter_context(tc.tile_pool(name="consts", bufs=1))
+        xpool = ctx.enter_context(tc.tile_pool(name="xpool", bufs=XBUFS))
+        gpool = ctx.enter_context(tc.tile_pool(name="gpool", bufs=3))
+        qpool = ctx.enter_context(tc.tile_pool(name="qpool", bufs=3))
+        zpool = ctx.enter_context(tc.tile_pool(name="zpool", bufs=4))
+        ppool = ctx.enter_context(tc.tile_pool(name="ppool", bufs=1))
+        epool = ctx.enter_context(tc.tile_pool(name="epool", bufs=3))
+        ps_t = ctx.enter_context(tc.psum_pool(name="ps_t", bufs=4))
+        ps_z = ctx.enter_context(tc.psum_pool(name="ps_z", bufs=4))
+        ctx.enter_context(tc.manual_schedule())
+
+        x_tiles = {}
+        bank_tiles = {}
+        xg_tiles = {}
+        code_tiles = {}
+        z_banks = {}
+        zs_tiles = {}
+        ig_tiles = {}
+        fc_tiles = {}
+        cn_tiles = {}
+        th_tiles = {}
+        hn_tiles = {}
+
+        def load_x(c, parts):
+            x_sb = xpool.tile([P, TC * I], BF16, name="x_sb")
+            step = TC // parts
+            for k in range(parts):
+                nc.sync.dma_start(
+                    out=x_sb[:, k * step * I:(k + 1) * step * I],
+                    in_=inputs[:, c * TC + k * step:c * TC + (k + 1) * step, :].rearrange("b t k -> b (t k)"),
+                )
+            x_tiles[c] = x_sb
+
+        w_sb = consts.tile([P, 4 * I], BF16, name="w_sb")
+        for q in range(4):
+            nc.sync.dma_start(out=w_sb[:, q * I:(q + 1) * I], in_=w_in[q])
+        load_x(0, TC)
+        small = consts.tile([P, 5 * H], BF16, name="small")
+        nc.sync.dma_start(out=small[:, 0:H], in_=h0[0])
+        for q in range(4):
+            nc.sync.dma_start(out=small[:, (q + 1) * H:(q + 2) * H], in_=w_hid[q])
+        load_x(1, 1)
+        brow = consts.tile([P, G4], BF16, name="brow")
+        nc.vector.memset(brow[:].bitcast(I32), 0)
+        for q in range(4):
+            nc.sync.dma_start(out=brow[0:1, q * H:(q + 1) * H], in_=b_in[q].rearrange("h o -> o h"))
+            nc.sync.dma_start(out=brow[1:2, q * H:(q + 1) * H], in_=b_hid[q].rearrange("h o -> o h"))
+        c0_bf = consts.tile([P, H], BF16, name="c0_bf")
+        nc.sync.dma_start(out=c0_bf[:], in_=c0[0])
+        for c in range(2, XBUFS):
+            load_x(c, 1)
+
+        ident_f = consts.tile([P, P], F32, name="ident_f")
+        make_identity(nc, ident_f[:])
+        ident_b = consts.tile([P, P], BF16, name="ident_b")
+        make_identity(nc, ident_b[:])
+        ones = consts.tile([P, P], BF16, name="ones")
+        nc.vector.memset(ones[:], 1.0)
+        warm = consts.tile([P, 1], F32, name="warm")
+        nc.vector.memset(warm[:], 0.0)
+        warm_out = consts.tile([P, 1], F32, name="warm_out")
+        nc.scalar.activation(out=warm_out[:], in_=warm[:], func=ACT.Sigmoid)
+
+        def transpose_rows(words):
+            bank = ps_t.tile([P, 4 * P], F32, name="bank", tag="bank")
+            for s in range(4):
+                first = (s // 2) * 2 * P + s % 2
+                nc.tensor.transpose(bank[:, s * P:(s + 1) * P], words[:, first:first + 2 * P - 1:2], ident_f[:])
+            return bank
+
+        def copy_out(engine_copy, dst_words, bank):
+            engine_copy(out=dst_words, in_=bank[:].rearrange("p (g u c) -> p g c u", g=2, u=2, c=P))
+
+        wg = consts.tile([P, 2 * G4 * 4], BF16, name="wg", align_bytes=64)
+        wg_words = wg[:].bitcast(F32).rearrange("p (g c u) -> p g c u", g=2, c=G4, u=2)
+        w_words = w_sb[:].bitcast(F32)
+        for q in range(4):
+            bank = transpose_rows(w_words[:, q * 512:(q + 1) * 512])
+            copy_out(nc.vector.tensor_copy if q % 2 == 0 else nc.scalar.copy,
+                     wg_words[:, :, q * H:(q + 1) * H, :], bank)
+        w_codes = consts.tile([P, 2 * G4], U32, name="w_codes", align_bytes=64)
+        w_scales = consts.tile([P, 2 * G4], U8, name="w_scales", align_bytes=64)
+        nc.vector.quantize_mx(out=w_codes[:].bitcast(FP8X4), scales=w_scales[:], in_=wg[:])
+
+        r_sb = consts.tile([P, G4], F32, name="r_sb")
+        c0_f = consts.tile([P, H], F32, name="c0_f")
+
+        def make_r():
+            small_ps = ps_z.tile([P, 5 * H], BF16, name="small_ps", tag="z_ps")
+            for s in range(5):
+                nc.tensor.transpose(small_ps[:, s * H:(s + 1) * H], small[:, s * H:(s + 1) * H], ident_b[:])
+            small_t = consts.tile([P, 5 * H], BF16, name="small_t")
+            nc.vector.tensor_copy(out=small_t[:], in_=small_ps[:])
+            r_ps = ps_z.tile([P, G4], F32, name="r_ps", tag="z_ps")
+            nc.tensor.matmul(r_ps[:], lhsT=small_t[:, 0:H], rhs=small_t[:, H:5 * H], start=True, stop=False)
+            nc.tensor.matmul(r_ps[:], lhsT=ones[:], rhs=brow[:], start=False, stop=True)
+            nc.vector.tensor_copy(out=r_sb[:], in_=r_ps[:])
+            nc.vector.tensor_copy(out=c0_f[:], in_=c0_bf[:])
+
+        def stage_tp(c):
+            x_words = x_tiles[c][:].bitcast(F32)
+            bank_tiles[c] = [transpose_rows(x_words[:, j * 512:(j + 1) * 512]) for j in range(TC)]
+            if c + XBUFS < NCH:
+                load_x(c + XBUFS, 1)
+
+        def stage_copy(c, share_with_vector):
+            xg = gpool.tile([P, TC * 2 * P * 4], BF16, name="xg", align_bytes=64)
+            xg_words = xg[:].bitcast(F32).rearrange("p (j g c u) -> p j g c u", j=TC, g=2, c=P, u=2)
+            for j in range(TC):
+                on_vector = share_with_vector and j % 2 == 1
+                copy_out(nc.vector.tensor_copy if on_vector else nc.scalar.copy, xg_words[:, j], bank_tiles[c][j])
+            xg_tiles[c] = xg
+
+        def stage_q(c):
+            x_codes = qpool.tile([P, TC * 2 * P], U32, name="x_codes", align_bytes=64)
+            x_scales = qpool.tile([P, TC * 2 * P], U8, name="x_scales", align_bytes=64)
+            nc.vector.quantize_mx(out=x_codes[:].bitcast(FP8X4), scales=x_scales[:], in_=xg_tiles[c][:])
+            code_tiles[c] = (x_codes, x_scales)
+
+        def stage_mx(c):
+            x_codes, x_scales = code_tiles[c]
+            banks = []
+            for j in range(TC):
+                z_ps = ps_z.tile([P, G4], F32, name="z_ps", tag="z_ps")
+                for g in range(2):
+                    cols = slice((j * 2 + g) * P, (j * 2 + g + 1) * P)
+                    nc.tensor.matmul_mx(
+                        out=z_ps[:],
+                        lhsT=x_codes[:, cols].bitcast(FP8X4),
+                        lhsT_scale=x_scales[:, cols],
+                        rhs=w_codes[:, g * G4:(g + 1) * G4].bitcast(FP8X4),
+                        rhs_scale=w_scales[:, g * G4:(g + 1) * G4],
+                        start=(g == 0),
+                        stop=(g == 1),
+                    )
+                banks.append(z_ps)
+            z_banks[c] = banks
+
+        def stage_add_r(c):
+            zs = zpool.tile([P, TC, G4], F32, name="zs")
+            for j in range(TC):
+                nc.vector.tensor_tensor(out=zs[:, j, :], in0=z_banks[c][j][:], in1=r_sb[:], op=ALU.add)
+            zs_tiles[c] = zs
+
+        def stage_act(c, span):
+            js = slice(span[0], span[1])
+            zs = zs_tiles[c]
+            nc.scalar.activation(out=zs[:, js, 0:3 * H], in_=zs[:, js, 0:3 * H], func=ACT.Sigmoid)
+            nc.scalar.activation(out=zs[:, js, 3 * H:G4], in_=zs[:, js, 3 * H:G4], func=ACT.Tanh)
+
+        def stage_products(c, span, engine):
+            js = slice(span[0], span[1])
+            zs = zs_tiles[c]
+            if c not in ig_tiles:
+                ig_tiles[c] = ppool.tile([P, TC, H], F32, name="ig")
+                fc_tiles[c] = ppool.tile([P, TC, H], F32, name="fc")
+            n = span[1] - span[0]
+            engine.tensor_tensor(out=ig_tiles[c][:, js, :], in0=zs[:, js, 0:H], in1=zs[:, js, 3 * H:G4], op=ALU.mult)
+            engine.tensor_tensor(out=fc_tiles[c][:, js, :], in0=zs[:, js, H:2 * H],
+                                 in1=c0_f[:].unsqueeze(1).to_broadcast([P, n, H]), op=ALU.mult)
+
+        def stage_sum(c, span):
+            js = slice(span[0], span[1])
+            if c not in cn_tiles:
+                cn_tiles[c] = epool.tile([P, TC, H], F32, name="cn")
+            nc.vector.tensor_tensor(out=cn_tiles[c][:, js, :], in0=fc_tiles[c][:, js, :], in1=ig_tiles[c][:, js, :],
+                                    op=ALU.add)
+
+        def stage_tanh_c(c, span):
+            js = slice(span[0], span[1])
+            if c not in th_tiles:
+                th_tiles[c] = epool.tile([P, TC, H], F32, name="th")
+            nc.scalar.activation(out=th_tiles[c][:, js, :], in_=cn_tiles[c][:, js, :], func=ACT.Tanh)
+
+        def stage_out(c, span):
+            js = slice(span[0], span[1])
+            if c not in hn_tiles:
+                hn_tiles[c] = epool.tile([P, TC, H], F32, name="hn")
+            hn = hn_tiles[c]
+            nc.vector.tensor_tensor(out=hn[:, js, :], in0=zs_tiles[c][:, js, 2 * H:3 * H], in1=th_tiles[c][:, js, :],
+                                    op=ALU.mult)
+            nc.sync.dma_start(out=out_0[c * TC + span[0]:c * TC + span[1]].rearrange("t b h -> b t h"),
+                              in_=hn[:, js, :])
+
+        def live(c):
+            return 0 <= c < NCH
+
+        whole = (0, TC)
+
+        stage_tp(0)
+        stage_copy(0, True)
+        stage_q(0)
+        stage_tp(1)
+        stage_copy(1, True)
+        make_r()
+
+        for i in range(NCH):
+            stage_mx(i)
+            if live(i + 2):
+                stage_tp(i + 2)
+            if live(i - 1):
+                stage_act(i - 1, whole)
+            if live(i + 1):
+                stage_q(i + 1)
+            if live(i - 3):
+                stage_out(i - 3, whole)
+            if live(i - 2):
+                stage_sum(i - 2, whole)
+            if live(i - 1):
+                stage_products(i - 1, whole, nc.gpsimd)
+            stage_add_r(i)
+            if live(i + 2):
+                stage_copy(i + 2, False)
+            if live(i - 2):
+                stage_tanh_c(i - 2, whole)
+
+        last = NCH - 1
+        halves = [(0, TC // 2), (TC // 2, TC)]
+        for js in halves:
+            stage_act(last, js)
+        stage_sum(last - 1, whole)
+        stage_tanh_c(last - 1, whole)
+        stage_out(last - 2, whole)
+        for js in halves:
+            stage_products(last, js, nc.vector)
+            stage_sum(last, js)
+            stage_tanh_c(last, js)
+            if js[0] == 0:
+                stage_out(last - 1, whole)
+        nc.sync.dma_start(out=out_2[0], in_=cn_tiles[last][:, TC - 1, :])
+        for js in halves:
+            stage_out(last, js)
+        nc.sync.dma_start(out=out_1[0], in_=hn_tiles[last][:, TC - 1, :])

@@ -17,6 +17,7 @@ P = 128
 G4 = 4 * H
 TC = 4
 NCH = T // TC
+IG_TILES = 2
 XBUFS = 8
 FLOPS = 2 * B * T * I * G4 + 2 * B * H * G4
 
@@ -50,6 +51,7 @@ def tile_naivelstm_pa_t_kernel(
         z_banks = {}
         zs_tiles = {}
         ig_tiles = {}
+        igv_tiles = {}
         fc_tiles = {}
         cn_tiles = {}
         th_tiles = {}
@@ -65,29 +67,41 @@ def tile_naivelstm_pa_t_kernel(
                 )
             x_tiles[c] = x_sb
 
-        w_sb = consts.tile([P, 4 * I], BF16, name="w_sb")
-        for q in range(4):
-            nc.sync.dma_start(out=w_sb[:, q * I:(q + 1) * I], in_=w_in[q])
-        load_x(0, TC)
-        small = consts.tile([P, 5 * H], BF16, name="small")
-        nc.sync.dma_start(out=small[:, 0:H], in_=h0[0])
-        for q in range(4):
-            nc.sync.dma_start(out=small[:, (q + 1) * H:(q + 2) * H], in_=w_hid[q])
-        load_x(1, 1)
-        brow = consts.tile([P, G4], BF16, name="brow")
-        nc.vector.memset(brow[:].bitcast(I32), 0)
-        for q in range(4):
-            nc.sync.dma_start(out=brow[0:1, q * H:(q + 1) * H], in_=b_in[q].rearrange("h o -> o h"))
-            nc.sync.dma_start(out=brow[1:2, q * H:(q + 1) * H], in_=b_hid[q].rearrange("h o -> o h"))
-        c0_bf = consts.tile([P, H], BF16, name="c0_bf")
-        nc.sync.dma_start(out=c0_bf[:], in_=c0[0])
-        for c in range(2, XBUFS):
-            load_x(c, 1)
-
         ident_f = consts.tile([P, P], F32, name="ident_f")
         make_identity(nc, ident_f[:])
         ident_b = consts.tile([P, P], BF16, name="ident_b")
         make_identity(nc, ident_b[:])
+        small = consts.tile([P, 5 * H], BF16, name="small")
+        w_sb = consts.tile([P, 4 * I], BF16, name="w_sb")
+        brow = consts.tile([P, G4], BF16, name="brow")
+        nc.vector.memset(brow[:].bitcast(I32), 0)
+        c0_bf = consts.tile([P, H], BF16, name="c0_bf")
+
+        def load_small(queue, s):
+            queue.dma_start(out=small[:, s * H:(s + 1) * H], in_=h0[0] if s == 0 else w_hid[s - 1])
+
+        def load_bias(queue, q, row):
+            source = b_in[q] if row == 0 else b_hid[q]
+            queue.dma_start(out=brow[row:row + 1, q * H:(q + 1) * H], in_=source.rearrange("h o -> o h"))
+
+        for s in range(4):
+            load_small(nc.scalar, s)
+        for q in range(4):
+            nc.sync.dma_start(out=w_sb[:, q * I:(q + 1) * I], in_=w_in[q])
+        load_x(0, 2)
+        load_bias(nc.sync, 0, 0)
+        load_bias(nc.sync, 0, 1)
+        load_bias(nc.sync, 1, 0)
+        load_x(1, 2)
+        load_small(nc.gpsimd, 4)
+        load_bias(nc.gpsimd, 1, 1)
+        for q in range(2, 4):
+            load_bias(nc.gpsimd, q, 0)
+            load_bias(nc.gpsimd, q, 1)
+        nc.gpsimd.dma_start(out=c0_bf[:], in_=c0[0])
+        for c in range(2, XBUFS):
+            load_x(c, 1)
+
         ones = consts.tile([P, P], BF16, name="ones")
         nc.vector.memset(ones[:], 1.0)
         warm = consts.tile([P, 1], F32, name="warm")
@@ -108,73 +122,84 @@ def tile_naivelstm_pa_t_kernel(
         wg = consts.tile([P, 2 * G4 * 4], BF16, name="wg", align_bytes=64)
         wg_words = wg[:].bitcast(F32).rearrange("p (g c u) -> p g c u", g=2, c=G4, u=2)
         w_words = w_sb[:].bitcast(F32)
-        for q in range(4):
-            bank = transpose_rows(w_words[:, q * 512:(q + 1) * 512])
-            copy_out(nc.vector.tensor_copy if q % 2 == 0 else nc.scalar.copy,
-                     wg_words[:, :, q * H:(q + 1) * H, :], bank)
         w_codes = consts.tile([P, 2 * G4], U32, name="w_codes", align_bytes=64)
         w_scales = consts.tile([P, 2 * G4], U8, name="w_scales", align_bytes=64)
-        nc.vector.quantize_mx(out=w_codes[:].bitcast(FP8X4), scales=w_scales[:], in_=wg[:])
-
         r_sb = consts.tile([P, G4], F32, name="r_sb")
         c0_f = consts.tile([P, H], F32, name="c0_f")
+        nc.gpsimd.tensor_copy(out=c0_f[:], in_=c0_bf[:])
 
-        def make_r():
-            small_ps = ps_z.tile([P, 5 * H], BF16, name="small_ps", tag="z_ps")
+        def weights_tp(q):
+            bank_tiles["w", q] = transpose_rows(w_words[:, q * 512:(q + 1) * 512])
+
+        def weights_copy(q, engine_copy):
+            copy_out(engine_copy, wg_words[:, :, q * H:(q + 1) * H, :], bank_tiles["w", q])
+
+        def weights_quantise(q):
+            for g in range(2):
+                first = g * G4 + q * H
+                nc.vector.quantize_mx(out=w_codes[:, first:first + H].bitcast(FP8X4),
+                                      scales=w_scales[:, first:first + H],
+                                      in_=wg[:, first * 4:(first + H) * 4])
+
+        def r_transposes():
+            small_ps = ps_t.tile([P, 5 * H], BF16, name="small_ps", tag="bank")
             for s in range(5):
                 nc.tensor.transpose(small_ps[:, s * H:(s + 1) * H], small[:, s * H:(s + 1) * H], ident_b[:])
             small_t = consts.tile([P, 5 * H], BF16, name="small_t")
             nc.vector.tensor_copy(out=small_t[:], in_=small_ps[:])
-            r_ps = ps_z.tile([P, G4], F32, name="r_ps", tag="z_ps")
+            return small_t
+
+        def r_matmuls(small_t):
+            r_ps = ps_t.tile([P, G4], F32, name="r_ps", tag="bank")
             nc.tensor.matmul(r_ps[:], lhsT=small_t[:, 0:H], rhs=small_t[:, H:5 * H], start=True, stop=False)
             nc.tensor.matmul(r_ps[:], lhsT=ones[:], rhs=brow[:], start=False, stop=True)
-            nc.vector.tensor_copy(out=r_sb[:], in_=r_ps[:])
-            nc.vector.tensor_copy(out=c0_f[:], in_=c0_bf[:])
+            nc.scalar.copy(out=r_sb[:], in_=r_ps[:])
 
-        def stage_tp(c):
+        def stage_tp(c, j):
             x_words = x_tiles[c][:].bitcast(F32)
-            bank_tiles[c] = [transpose_rows(x_words[:, j * 512:(j + 1) * 512]) for j in range(TC)]
-            if c + XBUFS < NCH:
+            bank_tiles[c, j] = transpose_rows(x_words[:, j * 512:(j + 1) * 512])
+            if j == TC - 1 and c + XBUFS < NCH:
                 load_x(c + XBUFS, 1)
 
-        def stage_copy(c, share_with_vector):
-            xg = gpool.tile([P, TC * 2 * P * 4], BF16, name="xg", align_bytes=64)
-            xg_words = xg[:].bitcast(F32).rearrange("p (j g c u) -> p j g c u", j=TC, g=2, c=P, u=2)
-            for j in range(TC):
-                on_vector = share_with_vector and j % 2 == 1
-                copy_out(nc.vector.tensor_copy if on_vector else nc.scalar.copy, xg_words[:, j], bank_tiles[c][j])
-            xg_tiles[c] = xg
+        def stage_copy(c, j, engine_copy):
+            if c not in xg_tiles:
+                xg_tiles[c] = gpool.tile([P, TC * 2 * P * 4], BF16, name="xg", align_bytes=64)
+            xg_words = xg_tiles[c][:].bitcast(F32).rearrange("p (j g c u) -> p j g c u", j=TC, g=2, c=P, u=2)
+            copy_out(engine_copy, xg_words[:, j], bank_tiles[c, j])
 
-        def stage_q(c):
-            x_codes = qpool.tile([P, TC * 2 * P], U32, name="x_codes", align_bytes=64)
-            x_scales = qpool.tile([P, TC * 2 * P], U8, name="x_scales", align_bytes=64)
-            nc.vector.quantize_mx(out=x_codes[:].bitcast(FP8X4), scales=x_scales[:], in_=xg_tiles[c][:])
-            code_tiles[c] = (x_codes, x_scales)
-
-        def stage_mx(c):
+        def stage_q(c, span):
+            if c not in code_tiles:
+                x_codes = qpool.tile([P, TC * 2 * P], U32, name="x_codes", align_bytes=64)
+                x_scales = qpool.tile([P, TC * 2 * P], U8, name="x_scales", align_bytes=64)
+                code_tiles[c] = (x_codes, x_scales)
             x_codes, x_scales = code_tiles[c]
-            banks = []
-            for j in range(TC):
-                z_ps = ps_z.tile([P, G4], F32, name="z_ps", tag="z_ps")
-                for g in range(2):
-                    cols = slice((j * 2 + g) * P, (j * 2 + g + 1) * P)
-                    nc.tensor.matmul_mx(
-                        out=z_ps[:],
-                        lhsT=x_codes[:, cols].bitcast(FP8X4),
-                        lhsT_scale=x_scales[:, cols],
-                        rhs=w_codes[:, g * G4:(g + 1) * G4].bitcast(FP8X4),
-                        rhs_scale=w_scales[:, g * G4:(g + 1) * G4],
-                        start=(g == 0),
-                        stop=(g == 1),
-                    )
-                banks.append(z_ps)
-            z_banks[c] = banks
+            cols = slice(span[0] * 2 * P, span[1] * 2 * P)
+            nc.vector.quantize_mx(out=x_codes[:, cols].bitcast(FP8X4), scales=x_scales[:, cols],
+                                  in_=xg_tiles[c][:, span[0] * 8 * P:span[1] * 8 * P])
 
-        def stage_add_r(c):
-            zs = zpool.tile([P, TC, G4], F32, name="zs")
-            for j in range(TC):
-                nc.vector.tensor_tensor(out=zs[:, j, :], in0=z_banks[c][j][:], in1=r_sb[:], op=ALU.add)
-            zs_tiles[c] = zs
+        def stage_mx(c, j):
+            x_codes, x_scales = code_tiles[c]
+            if c < NCH - 1:
+                z_ps = ps_z.tile([P, G4], F32, name="z_ps", tag="z_ps")
+            else:
+                z_ps = ps_t.tile([P, G4], F32, name="bank", tag="bank")
+            for g in range(2):
+                cols = slice((j * 2 + g) * P, (j * 2 + g + 1) * P)
+                nc.tensor.matmul_mx(
+                    out=z_ps[:],
+                    lhsT=x_codes[:, cols].bitcast(FP8X4),
+                    lhsT_scale=x_scales[:, cols],
+                    rhs=w_codes[:, g * G4:(g + 1) * G4].bitcast(FP8X4),
+                    rhs_scale=w_scales[:, g * G4:(g + 1) * G4],
+                    start=(g == 0),
+                    stop=(g == 1),
+                )
+            z_banks[c, j] = z_ps
+
+        def stage_add_r(c, j):
+            if c not in zs_tiles:
+                zs_tiles[c] = zpool.tile([P, TC, G4], F32, name="zs")
+            nc.vector.tensor_tensor(out=zs_tiles[c][:, j, :], in0=z_banks[c, j][:], in1=r_sb[:], op=ALU.add)
 
         def stage_act(c, span):
             js = slice(span[0], span[1])
@@ -182,23 +207,45 @@ def tile_naivelstm_pa_t_kernel(
             nc.scalar.activation(out=zs[:, js, 0:3 * H], in_=zs[:, js, 0:3 * H], func=ACT.Sigmoid)
             nc.scalar.activation(out=zs[:, js, 3 * H:G4], in_=zs[:, js, 3 * H:G4], func=ACT.Tanh)
 
-        def stage_products(c, span, engine):
+        def product_ig(c, span, engine, tile):
             js = slice(span[0], span[1])
             zs = zs_tiles[c]
-            if c not in ig_tiles:
-                ig_tiles[c] = ppool.tile([P, TC, H], F32, name="ig")
-                fc_tiles[c] = ppool.tile([P, TC, H], F32, name="fc")
+            engine.tensor_tensor(out=tile[:, js, :], in0=zs[:, js, 0:H], in1=zs[:, js, 3 * H:G4], op=ALU.mult)
+
+        def product_fc(c, span, engine, tile):
+            js = slice(span[0], span[1])
             n = span[1] - span[0]
-            engine.tensor_tensor(out=ig_tiles[c][:, js, :], in0=zs[:, js, 0:H], in1=zs[:, js, 3 * H:G4], op=ALU.mult)
-            engine.tensor_tensor(out=fc_tiles[c][:, js, :], in0=zs[:, js, H:2 * H],
+            engine.tensor_tensor(out=tile[:, js, :], in0=zs_tiles[c][:, js, H:2 * H],
                                  in1=c0_f[:].unsqueeze(1).to_broadcast([P, n, H]), op=ALU.mult)
 
+        def stage_ig_vector(c):
+            igv_tiles[c] = epool.tile([P, TC, H], F32, name="igv")
+            product_ig(c, (IG_TILES, TC), nc.vector, igv_tiles[c])
+
+        def stage_gpsimd(c):
+            fc_tiles[c] = ppool.tile([P, TC, H], F32, name="fc")
+            product_fc(c, (0, TC), nc.gpsimd, fc_tiles[c])
+            if IG_TILES:
+                ig_tiles[c] = ppool.tile([P, TC, H], F32, name="ig")
+                product_ig(c, (0, IG_TILES), nc.gpsimd, ig_tiles[c])
+
+        def stage_products_vector(c, span):
+            if c not in igv_tiles:
+                igv_tiles[c] = epool.tile([P, TC, H], F32, name="igv")
+                fc_tiles[c] = epool.tile([P, TC, H], F32, name="fcv")
+            product_ig(c, span, nc.vector, igv_tiles[c])
+            product_fc(c, span, nc.vector, fc_tiles[c])
+
         def stage_sum(c, span):
-            js = slice(span[0], span[1])
             if c not in cn_tiles:
                 cn_tiles[c] = epool.tile([P, TC, H], F32, name="cn")
-            nc.vector.tensor_tensor(out=cn_tiles[c][:, js, :], in0=fc_tiles[c][:, js, :], in1=ig_tiles[c][:, js, :],
-                                    op=ALU.add)
+            split = IG_TILES if c in ig_tiles else 0
+            parts = [(span[0], min(span[1], split), ig_tiles), (max(span[0], split), span[1], igv_tiles)]
+            for lo, hi, source in parts:
+                if lo < hi:
+                    js = slice(lo, hi)
+                    nc.vector.tensor_tensor(out=cn_tiles[c][:, js, :], in0=fc_tiles[c][:, js, :],
+                                            in1=source[c][:, js, :], op=ALU.add)
 
         def stage_tanh_c(c, span):
             js = slice(span[0], span[1])
@@ -220,35 +267,67 @@ def tile_naivelstm_pa_t_kernel(
             return 0 <= c < NCH
 
         whole = (0, TC)
+        last = NCH - 1
+        on_scalar, on_vector = nc.scalar.copy, nc.vector.tensor_copy
 
-        stage_tp(0)
-        stage_copy(0, True)
-        stage_q(0)
-        stage_tp(1)
-        stage_copy(1, True)
-        make_r()
+        for q in range(4):
+            weights_tp(q)
+            weights_copy(q, on_scalar)
+            weights_quantise(q)
+        small_t = r_transposes()
+        for j in range(TC):
+            stage_tp(0, j)
+            stage_copy(0, j, on_vector if j % 2 == 0 else on_scalar)
+            if j > 0:
+                stage_q(0, (j - 1, j))
+        stage_q(0, (TC - 1, TC))
+        r_matmuls(small_t)
+        for j in range(TC):
+            stage_tp(1, j)
+            stage_copy(1, j, on_scalar if j < 2 else on_vector)
+        stage_q(1, (0, 2))
+        for j in range(TC):
+            stage_mx(0, j)
+        for j in range(2):
+            stage_add_r(0, j)
+        stage_q(1, (2, 4))
+        for j in range(2, 4):
+            stage_add_r(0, j)
 
-        for i in range(NCH):
-            stage_mx(i)
-            if live(i + 2):
-                stage_tp(i + 2)
-            if live(i - 1):
+        for j in range(TC):
+            stage_tp(2, j)
+        stage_act(0, whole)
+        for j in range(TC):
+            stage_copy(2, j, on_vector)
+
+        for i in range(1, NCH):
+            for pair in ((0, 1), (2, 3)):
+                for j in pair:
+                    stage_mx(i, j)
+                for j in pair:
+                    if live(i + 2):
+                        stage_tp(i + 2, j)
+            if i > 1:
                 stage_act(i - 1, whole)
             if live(i + 1):
-                stage_q(i + 1)
+                stage_q(i + 1, whole)
             if live(i - 3):
                 stage_out(i - 3, whole)
             if live(i - 2):
                 stage_sum(i - 2, whole)
-            if live(i - 1):
-                stage_products(i - 1, whole, nc.gpsimd)
-            stage_add_r(i)
+            if i > 1:
+                stage_gpsimd(i - 1)
+            for j in range(TC):
+                stage_add_r(i, j)
+            if i == 1:
+                stage_products_vector(0, whole)
+            elif IG_TILES < TC:
+                stage_ig_vector(i - 1)
             if live(i + 2):
-                stage_copy(i + 2, False)
+                for j in range(TC):
+                    stage_copy(i + 2, j, on_scalar)
             if live(i - 2):
                 stage_tanh_c(i - 2, whole)
-
-        last = NCH - 1
         halves = [(0, TC // 2), (TC // 2, TC)]
         for js in halves:
             stage_act(last, js)
@@ -256,7 +335,7 @@ def tile_naivelstm_pa_t_kernel(
         stage_tanh_c(last - 1, whole)
         stage_out(last - 2, whole)
         for js in halves:
-            stage_products(last, js, nc.vector)
+            stage_products_vector(last, js)
             stage_sum(last, js)
             stage_tanh_c(last, js)
             if js[0] == 0:

@@ -17,7 +17,7 @@ P = 128
 G4 = 4 * H
 TC = 4
 NCH = T // TC
-IG_TILES = 2
+IG_TILES = 1
 XBUFS = 8
 FLOPS = 2 * B * T * I * G4 + 2 * B * H * G4
 
@@ -232,7 +232,7 @@ def tile_naivelstm_pa_t_kernel(
         def stage_products_vector(c, span):
             if c not in igv_tiles:
                 igv_tiles[c] = epool.tile([P, TC, H], F32, name="igv")
-                fc_tiles[c] = epool.tile([P, TC, H], F32, name="fcv")
+                fc_tiles[c] = ppool.tile([P, TC, H], F32, name="fc")
             product_ig(c, span, nc.vector, igv_tiles[c])
             product_fc(c, span, nc.vector, fc_tiles[c])
 
@@ -270,6 +270,39 @@ def tile_naivelstm_pa_t_kernel(
         last = NCH - 1
         on_scalar, on_vector = nc.scalar.copy, nc.vector.tensor_copy
 
+        NH = 2 * NCH
+        LEAD = 3
+
+        def pair(n):
+            return (n // 2, (2 * (n % 2), 2 * (n % 2) + 1))
+
+        def half_tp(n):
+            if n < NH:
+                c, js = pair(n)
+                for j in js:
+                    stage_tp(c, j)
+
+        def half_mx(n):
+            c, js = pair(n)
+            for j in js:
+                stage_mx(c, j)
+
+        def half_copy(n, e0, e1):
+            if n < NH:
+                c, js = pair(n)
+                stage_copy(c, js[0], e0)
+                stage_copy(c, js[1], e1)
+
+        def half_q(n):
+            if n < NH:
+                c, js = pair(n)
+                stage_q(c, (js[0], js[1] + 1))
+
+        def half_add(n):
+            c, js = pair(n)
+            for j in js:
+                stage_add_r(c, j)
+
         for q in range(4):
             weights_tp(q)
             weights_copy(q, on_scalar)
@@ -282,52 +315,48 @@ def tile_naivelstm_pa_t_kernel(
                 stage_q(0, (j - 1, j))
         stage_q(0, (TC - 1, TC))
         r_matmuls(small_t)
-        for j in range(TC):
-            stage_tp(1, j)
-            stage_copy(1, j, on_scalar if j < 2 else on_vector)
-        stage_q(1, (0, 2))
-        for j in range(TC):
-            stage_mx(0, j)
-        for j in range(2):
-            stage_add_r(0, j)
-        stage_q(1, (2, 4))
-        for j in range(2, 4):
-            stage_add_r(0, j)
-
-        for j in range(TC):
-            stage_tp(2, j)
+        half_mx(0)
+        half_tp(2)
+        half_mx(1)
+        half_tp(3)
+        half_add(0)
+        half_copy(2, on_scalar, on_scalar)
+        half_add(1)
+        half_q(2)
+        half_copy(3, on_vector, on_vector)
+        half_q(3)
         stage_act(0, whole)
-        for j in range(TC):
-            stage_copy(2, j, on_vector)
+        half_tp(4)
 
         for i in range(1, NCH):
-            for pair in ((0, 1), (2, 3)):
-                for j in pair:
-                    stage_mx(i, j)
-                for j in pair:
-                    if live(i + 2):
-                        stage_tp(i + 2, j)
+            half_mx(2 * i)
+            half_tp(2 * i + LEAD)
+            half_mx(2 * i + 1)
+            half_tp(2 * i + 1 + LEAD)
+            if i == 1:
+                half_copy(4, on_scalar, on_vector)
+                half_q(4)
             if i > 1:
                 stage_act(i - 1, whole)
-            if live(i + 1):
-                stage_q(i + 1, whole)
+            if i > 1:
+                half_q(2 * i + 2)
             if live(i - 3):
                 stage_out(i - 3, whole)
             if live(i - 2):
                 stage_sum(i - 2, whole)
             if i > 1:
                 stage_gpsimd(i - 1)
-            for j in range(TC):
-                stage_add_r(i, j)
-            if i == 1:
-                stage_products_vector(0, whole)
-            elif IG_TILES < TC:
-                stage_ig_vector(i - 1)
-            if live(i + 2):
-                for j in range(TC):
-                    stage_copy(i + 2, j, on_scalar)
+            half_add(2 * i)
+            half_add(2 * i + 1)
+            half_copy(2 * i + LEAD, on_scalar, on_scalar)
+            half_copy(2 * i + LEAD + 1, on_scalar, on_scalar)
             if live(i - 2):
                 stage_tanh_c(i - 2, whole)
+            half_q(2 * i + LEAD)
+            if i == 1:
+                stage_products_vector(0, whole)
+            else:
+                stage_ig_vector(i - 1)
         halves = [(0, TC // 2), (TC // 2, TC)]
         for js in halves:
             stage_act(last, js)

@@ -119,11 +119,11 @@ def tile_naivelstm_pa_t_kernel(
         def copy_out(engine_copy, dst_words, bank):
             engine_copy(out=dst_words, in_=bank[:].rearrange("p (g u c) -> p g c u", g=2, u=2, c=P))
 
-        wg = consts.tile([P, 2 * G4 * 4], BF16, name="wg", align_bytes=64)
+        wg = consts.tile([P, 2 * G4 * 4], BF16, name="wg", align_bytes=256)
         wg_words = wg[:].bitcast(F32).rearrange("p (g c u) -> p g c u", g=2, c=G4, u=2)
         w_words = w_sb[:].bitcast(F32)
-        w_codes = consts.tile([P, 2 * G4], U32, name="w_codes", align_bytes=64)
-        w_scales = consts.tile([P, 2 * G4], U8, name="w_scales", align_bytes=64)
+        w_codes = consts.tile([P, 2 * G4], U32, name="w_codes", align_bytes=256)
+        w_scales = consts.tile([P, 2 * G4], U8, name="w_scales", align_bytes=256)
         r_sb = consts.tile([P, G4], F32, name="r_sb")
         c0_f = consts.tile([P, H], F32, name="c0_f")
         nc.gpsimd.tensor_copy(out=c0_f[:], in_=c0_bf[:])
@@ -163,14 +163,14 @@ def tile_naivelstm_pa_t_kernel(
 
         def stage_copy(c, j, engine_copy):
             if c not in xg_tiles:
-                xg_tiles[c] = gpool.tile([P, TC * 2 * P * 4], BF16, name="xg", align_bytes=64)
+                xg_tiles[c] = gpool.tile([P, TC * 2 * P * 4], BF16, name="xg", align_bytes=256)
             xg_words = xg_tiles[c][:].bitcast(F32).rearrange("p (j g c u) -> p j g c u", j=TC, g=2, c=P, u=2)
             copy_out(engine_copy, xg_words[:, j], bank_tiles[c, j])
 
         def stage_q(c, span):
             if c not in code_tiles:
-                x_codes = qpool.tile([P, TC * 2 * P], U32, name="x_codes", align_bytes=64)
-                x_scales = qpool.tile([P, TC * 2 * P], U8, name="x_scales", align_bytes=64)
+                x_codes = qpool.tile([P, TC * 2 * P], U32, name="x_codes", align_bytes=256)
+                x_scales = qpool.tile([P, TC * 2 * P], U8, name="x_scales", align_bytes=256)
                 code_tiles[c] = (x_codes, x_scales)
             x_codes, x_scales = code_tiles[c]
             cols = slice(span[0] * 2 * P, span[1] * 2 * P)
@@ -348,10 +348,10 @@ def tile_naivelstm_pa_t_kernel(
                 stage_gpsimd(i - 1)
             half_add(2 * i)
             half_add(2 * i + 1)
-            half_copy(2 * i + LEAD, on_scalar, on_scalar)
-            half_copy(2 * i + LEAD + 1, on_scalar, on_scalar)
             if live(i - 2):
                 stage_tanh_c(i - 2, whole)
+            half_copy(2 * i + LEAD, on_scalar, on_scalar)
+            half_copy(2 * i + LEAD + 1, on_scalar, on_scalar)
             half_q(2 * i + LEAD)
             if i == 1:
                 stage_products_vector(0, whole)
@@ -360,15 +360,16 @@ def tile_naivelstm_pa_t_kernel(
         halves = [(0, TC // 2), (TC // 2, TC)]
         for js in halves:
             stage_act(last, js)
+        stage_out(last - 2, whole)
         stage_sum(last - 1, whole)
         stage_tanh_c(last - 1, whole)
-        stage_out(last - 2, whole)
         for js in halves:
             stage_products_vector(last, js)
-            stage_sum(last, js)
-            stage_tanh_c(last, js)
-            if js[0] == 0:
-                stage_out(last - 1, whole)
+        stage_sum(last, halves[0])
+        stage_tanh_c(last, halves[0])
+        stage_out(last - 1, whole)
+        stage_sum(last, halves[1])
+        stage_tanh_c(last, halves[1])
         nc.sync.dma_start(out=out_2[0], in_=cn_tiles[last][:, TC - 1, :])
         for js in halves:
             stage_out(last, js)

@@ -17,7 +17,7 @@ P = 128
 G4 = 4 * H
 TC = 4
 NCH = T // TC
-IG_TILES = 1
+IG_TILES = 2
 XBUFS = 8
 FLOPS = 2 * B * T * I * G4 + 2 * B * H * G4
 
@@ -323,9 +323,8 @@ def tile_naivelstm_pa_t_kernel(
         half_copy(2, on_scalar, on_scalar)
         half_add(1)
         half_q(2)
-        half_copy(3, on_vector, on_vector)
+        half_copy(3, on_scalar, on_scalar)
         half_q(3)
-        stage_act(0, whole)
         half_tp(4)
 
         for i in range(1, NCH):
@@ -334,8 +333,9 @@ def tile_naivelstm_pa_t_kernel(
             half_mx(2 * i + 1)
             half_tp(2 * i + 1 + LEAD)
             if i == 1:
-                half_copy(4, on_scalar, on_vector)
+                half_copy(4, on_scalar, on_scalar)
                 half_q(4)
+                stage_act(0, whole)
             if i > 1:
                 stage_act(i - 1, whole)
             if i > 1:
@@ -373,4 +373,4 @@ def tile_naivelstm_pa_t_kernel(
         nc.sync.dma_start(out=out_2[0], in_=cn_tiles[last][:, TC - 1, :])
         for js in halves:
             stage_out(last, js)
-        nc.sync.dma_start(out=out_1[0], in_=hn_tiles[last][:, TC - 1, :])
+        nc.scalar.dma_start(out=out_1[0], in_=hn_tiles[last][:, TC - 1, :])

from contextlib import ExitStack

import concourse.mybir as mybir
from concourse.masks import make_identity

FP8X4 = mybir.dt.float8_e4m3fn_x4
BF16 = mybir.dt.bfloat16
F32 = mybir.dt.float32
I32 = mybir.dt.int32
U32 = mybir.dt.uint32
U8 = mybir.dt.uint8
ACT = mybir.ActivationFunctionType
ALU = mybir.AluOpType

B, T, I, H = 128, 64, 1024, 128
P = 128
G4 = 4 * H
TC = 4
NCH = T // TC
IG_TILES = 2
XBUFS = 8
FLOPS = 2 * B * T * I * G4 + 2 * B * H * G4


def tile_naivelstm_pa_t_kernel(
    tc, inputs, h0, c0, w_ii, b_ii, w_hi, b_hi, w_if_, b_if_, w_hf, b_hf,
    w_io, b_io, w_ho, b_ho, w_ig, b_ig, w_hg, b_hg, out_0, out_1, out_2,
):
    nc = tc.nc
    w_in = [w_ii, w_if_, w_io, w_ig]
    w_hid = [w_hi, w_hf, w_ho, w_hg]
    b_in = [b_ii, b_if_, b_io, b_ig]
    b_hid = [b_hi, b_hf, b_ho, b_hg]

    with ExitStack() as ctx:
        consts = ctx.enter_context(tc.tile_pool(name="consts", bufs=1))
        xpool = ctx.enter_context(tc.tile_pool(name="xpool", bufs=XBUFS))
        gpool = ctx.enter_context(tc.tile_pool(name="gpool", bufs=3))
        qpool = ctx.enter_context(tc.tile_pool(name="qpool", bufs=3))
        zpool = ctx.enter_context(tc.tile_pool(name="zpool", bufs=4))
        ppool = ctx.enter_context(tc.tile_pool(name="ppool", bufs=1))
        epool = ctx.enter_context(tc.tile_pool(name="epool", bufs=3))
        ps_t = ctx.enter_context(tc.psum_pool(name="ps_t", bufs=4))
        ps_z = ctx.enter_context(tc.psum_pool(name="ps_z", bufs=4))
        ctx.enter_context(tc.manual_schedule())

        x_tiles = {}
        bank_tiles = {}
        xg_tiles = {}
        code_tiles = {}
        z_banks = {}
        zs_tiles = {}
        ig_tiles = {}
        igv_tiles = {}
        fc_tiles = {}
        cn_tiles = {}
        th_tiles = {}
        hn_tiles = {}

        def load_x(c, parts):
            x_sb = xpool.tile([P, TC * I], BF16, name="x_sb")
            step = TC // parts
            for k in range(parts):
                nc.sync.dma_start(
                    out=x_sb[:, k * step * I:(k + 1) * step * I],
                    in_=inputs[:, c * TC + k * step:c * TC + (k + 1) * step, :].rearrange("b t k -> b (t k)"),
                )
            x_tiles[c] = x_sb

        ident_f = consts.tile([P, P], F32, name="ident_f")
        make_identity(nc, ident_f[:])
        ident_b = consts.tile([P, P], BF16, name="ident_b")
        make_identity(nc, ident_b[:])
        small = consts.tile([P, 5 * H], BF16, name="small")
        w_sb = consts.tile([P, 4 * I], BF16, name="w_sb")
        brow = consts.tile([P, G4], BF16, name="brow")
        nc.vector.memset(brow[:].bitcast(I32), 0)
        c0_bf = consts.tile([P, H], BF16, name="c0_bf")

        def load_small(queue, s):
            queue.dma_start(out=small[:, s * H:(s + 1) * H], in_=h0[0] if s == 0 else w_hid[s - 1])

        def load_bias(queue, q, row):
            source = b_in[q] if row == 0 else b_hid[q]
            queue.dma_start(out=brow[row:row + 1, q * H:(q + 1) * H], in_=source.rearrange("h o -> o h"))

        for s in range(4):
            load_small(nc.scalar, s)
        for q in range(4):
            nc.sync.dma_start(out=w_sb[:, q * I:(q + 1) * I], in_=w_in[q])
        load_x(0, 2)
        load_bias(nc.sync, 0, 0)
        load_bias(nc.sync, 0, 1)
        load_bias(nc.sync, 1, 0)
        load_x(1, 2)
        load_small(nc.gpsimd, 4)
        load_bias(nc.gpsimd, 1, 1)
        for q in range(2, 4):
            load_bias(nc.gpsimd, q, 0)
            load_bias(nc.gpsimd, q, 1)
        nc.gpsimd.dma_start(out=c0_bf[:], in_=c0[0])
        for c in range(2, XBUFS):
            load_x(c, 1)

        ones = consts.tile([P, P], BF16, name="ones")
        nc.vector.memset(ones[:], 1.0)
        warm = consts.tile([P, 1], F32, name="warm")
        nc.vector.memset(warm[:], 0.0)
        warm_out = consts.tile([P, 1], F32, name="warm_out")
        nc.scalar.activation(out=warm_out[:], in_=warm[:], func=ACT.Sigmoid)

        def transpose_rows(words):
            bank = ps_t.tile([P, 4 * P], F32, name="bank", tag="bank")
            for s in range(4):
                first = (s // 2) * 2 * P + s % 2
                nc.tensor.transpose(bank[:, s * P:(s + 1) * P], words[:, first:first + 2 * P - 1:2], ident_f[:])
            return bank

        def copy_out(engine_copy, dst_words, bank):
            engine_copy(out=dst_words, in_=bank[:].rearrange("p (g u c) -> p g c u", g=2, u=2, c=P))

        wg = consts.tile([P, 2 * G4 * 4], BF16, name="wg", align_bytes=256)
        wg_words = wg[:].bitcast(F32).rearrange("p (g c u) -> p g c u", g=2, c=G4, u=2)
        w_words = w_sb[:].bitcast(F32)
        w_codes = consts.tile([P, 2 * G4], U32, name="w_codes", align_bytes=256)
        w_scales = consts.tile([P, 2 * G4], U8, name="w_scales", align_bytes=256)
        r_sb = consts.tile([P, G4], F32, name="r_sb")
        c0_f = consts.tile([P, H], F32, name="c0_f")
        nc.gpsimd.tensor_copy(out=c0_f[:], in_=c0_bf[:])

        def weights_tp(q):
            bank_tiles["w", q] = transpose_rows(w_words[:, q * 512:(q + 1) * 512])

        def weights_copy(q, engine_copy):
            copy_out(engine_copy, wg_words[:, :, q * H:(q + 1) * H, :], bank_tiles["w", q])

        def weights_quantise(q):
            for g in range(2):
                first = g * G4 + q * H
                nc.vector.quantize_mx(out=w_codes[:, first:first + H].bitcast(FP8X4),
                                      scales=w_scales[:, first:first + H],
                                      in_=wg[:, first * 4:(first + H) * 4])

        def r_transposes():
            small_ps = ps_t.tile([P, 5 * H], BF16, name="small_ps", tag="bank")
            for s in range(5):
                nc.tensor.transpose(small_ps[:, s * H:(s + 1) * H], small[:, s * H:(s + 1) * H], ident_b[:])
            small_t = consts.tile([P, 5 * H], BF16, name="small_t")
            nc.vector.tensor_copy(out=small_t[:], in_=small_ps[:])
            return small_t

        def r_matmuls(small_t):
            r_ps = ps_t.tile([P, G4], F32, name="r_ps", tag="bank")
            nc.tensor.matmul(r_ps[:], lhsT=small_t[:, 0:H], rhs=small_t[:, H:5 * H], start=True, stop=False)
            nc.tensor.matmul(r_ps[:], lhsT=ones[:], rhs=brow[:], start=False, stop=True)
            nc.scalar.copy(out=r_sb[:], in_=r_ps[:])

        def stage_tp(c, j):
            x_words = x_tiles[c][:].bitcast(F32)
            bank_tiles[c, j] = transpose_rows(x_words[:, j * 512:(j + 1) * 512])
            if j == TC - 1 and c + XBUFS < NCH:
                load_x(c + XBUFS, 1)

        def stage_copy(c, j, engine_copy):
            if c not in xg_tiles:
                xg_tiles[c] = gpool.tile([P, TC * 2 * P * 4], BF16, name="xg", align_bytes=256)
            xg_words = xg_tiles[c][:].bitcast(F32).rearrange("p (j g c u) -> p j g c u", j=TC, g=2, c=P, u=2)
            copy_out(engine_copy, xg_words[:, j], bank_tiles[c, j])

        def stage_q(c, span):
            if c not in code_tiles:
                x_codes = qpool.tile([P, TC * 2 * P], U32, name="x_codes", align_bytes=256)
                x_scales = qpool.tile([P, TC * 2 * P], U8, name="x_scales", align_bytes=256)
                code_tiles[c] = (x_codes, x_scales)
            x_codes, x_scales = code_tiles[c]
            cols = slice(span[0] * 2 * P, span[1] * 2 * P)
            nc.vector.quantize_mx(out=x_codes[:, cols].bitcast(FP8X4), scales=x_scales[:, cols],
                                  in_=xg_tiles[c][:, span[0] * 8 * P:span[1] * 8 * P])

        def stage_mx(c, j):
            x_codes, x_scales = code_tiles[c]
            if c < NCH - 1:
                z_ps = ps_z.tile([P, G4], F32, name="z_ps", tag="z_ps")
            else:
                z_ps = ps_t.tile([P, G4], F32, name="bank", tag="bank")
            for g in range(2):
                cols = slice((j * 2 + g) * P, (j * 2 + g + 1) * P)
                nc.tensor.matmul_mx(
                    out=z_ps[:],
                    lhsT=x_codes[:, cols].bitcast(FP8X4),
                    lhsT_scale=x_scales[:, cols],
                    rhs=w_codes[:, g * G4:(g + 1) * G4].bitcast(FP8X4),
                    rhs_scale=w_scales[:, g * G4:(g + 1) * G4],
                    start=(g == 0),
                    stop=(g == 1),
                )
            z_banks[c, j] = z_ps

        def stage_add_r(c, j):
            if c not in zs_tiles:
                zs_tiles[c] = zpool.tile([P, TC, G4], F32, name="zs")
            nc.vector.tensor_tensor(out=zs_tiles[c][:, j, :], in0=z_banks[c, j][:], in1=r_sb[:], op=ALU.add)

        def stage_act(c, span):
            js = slice(span[0], span[1])
            zs = zs_tiles[c]
            nc.scalar.activation(out=zs[:, js, 0:3 * H], in_=zs[:, js, 0:3 * H], func=ACT.Sigmoid)
            nc.scalar.activation(out=zs[:, js, 3 * H:G4], in_=zs[:, js, 3 * H:G4], func=ACT.Tanh)

        def product_ig(c, span, engine, tile):
            js = slice(span[0], span[1])
            zs = zs_tiles[c]
            engine.tensor_tensor(out=tile[:, js, :], in0=zs[:, js, 0:H], in1=zs[:, js, 3 * H:G4], op=ALU.mult)

        def product_fc(c, span, engine, tile):
            js = slice(span[0], span[1])
            n = span[1] - span[0]
            engine.tensor_tensor(out=tile[:, js, :], in0=zs_tiles[c][:, js, H:2 * H],
                                 in1=c0_f[:].unsqueeze(1).to_broadcast([P, n, H]), op=ALU.mult)

        def stage_ig_vector(c):
            igv_tiles[c] = epool.tile([P, TC, H], F32, name="igv")
            product_ig(c, (IG_TILES, TC), nc.vector, igv_tiles[c])

        def stage_gpsimd(c):
            fc_tiles[c] = ppool.tile([P, TC, H], F32, name="fc")
            product_fc(c, (0, TC), nc.gpsimd, fc_tiles[c])
            if IG_TILES:
                ig_tiles[c] = ppool.tile([P, TC, H], F32, name="ig")
                product_ig(c, (0, IG_TILES), nc.gpsimd, ig_tiles[c])

        def stage_products_vector(c, span):
            if c not in igv_tiles:
                igv_tiles[c] = epool.tile([P, TC, H], F32, name="igv")
                fc_tiles[c] = ppool.tile([P, TC, H], F32, name="fc")
            product_ig(c, span, nc.vector, igv_tiles[c])
            product_fc(c, span, nc.vector, fc_tiles[c])

        def stage_sum(c, span):
            if c not in cn_tiles:
                cn_tiles[c] = epool.tile([P, TC, H], F32, name="cn")
            split = IG_TILES if c in ig_tiles else 0
            parts = [(span[0], min(span[1], split), ig_tiles), (max(span[0], split), span[1], igv_tiles)]
            for lo, hi, source in parts:
                if lo < hi:
                    js = slice(lo, hi)
                    nc.vector.tensor_tensor(out=cn_tiles[c][:, js, :], in0=fc_tiles[c][:, js, :],
                                            in1=source[c][:, js, :], op=ALU.add)

        def stage_tanh_c(c, span):
            js = slice(span[0], span[1])
            if c not in th_tiles:
                th_tiles[c] = epool.tile([P, TC, H], F32, name="th")
            nc.scalar.activation(out=th_tiles[c][:, js, :], in_=cn_tiles[c][:, js, :], func=ACT.Tanh)

        def stage_out(c, span):
            js = slice(span[0], span[1])
            if c not in hn_tiles:
                hn_tiles[c] = epool.tile([P, TC, H], F32, name="hn")
            hn = hn_tiles[c]
            nc.vector.tensor_tensor(out=hn[:, js, :], in0=zs_tiles[c][:, js, 2 * H:3 * H], in1=th_tiles[c][:, js, :],
                                    op=ALU.mult)
            nc.sync.dma_start(out=out_0[c * TC + span[0]:c * TC + span[1]].rearrange("t b h -> b t h"),
                              in_=hn[:, js, :])

        def live(c):
            return 0 <= c < NCH

        whole = (0, TC)
        last = NCH - 1
        on_scalar, on_vector = nc.scalar.copy, nc.vector.tensor_copy

        NH = 2 * NCH
        LEAD = 3

        def pair(n):
            return (n // 2, (2 * (n % 2), 2 * (n % 2) + 1))

        def half_tp(n):
            if n < NH:
                c, js = pair(n)
                for j in js:
                    stage_tp(c, j)

        def half_mx(n):
            c, js = pair(n)
            for j in js:
                stage_mx(c, j)

        def half_copy(n, e0, e1):
            if n < NH:
                c, js = pair(n)
                stage_copy(c, js[0], e0)
                stage_copy(c, js[1], e1)

        def half_q(n):
            if n < NH:
                c, js = pair(n)
                stage_q(c, (js[0], js[1] + 1))

        def half_add(n):
            c, js = pair(n)
            for j in js:
                stage_add_r(c, j)

        for q in range(4):
            weights_tp(q)
            weights_copy(q, on_scalar)
            weights_quantise(q)
        small_t = r_transposes()
        for j in range(TC):
            stage_tp(0, j)
            stage_copy(0, j, on_vector if j % 2 == 0 else on_scalar)
            if j > 0:
                stage_q(0, (j - 1, j))
        stage_q(0, (TC - 1, TC))
        r_matmuls(small_t)
        half_mx(0)
        half_tp(2)
        half_mx(1)
        half_tp(3)
        half_add(0)
        half_copy(2, on_scalar, on_scalar)
        half_add(1)
        half_q(2)
        half_copy(3, on_scalar, on_scalar)
        half_q(3)
        half_tp(4)

        for i in range(1, NCH):
            half_mx(2 * i)
            half_tp(2 * i + LEAD)
            half_mx(2 * i + 1)
            half_tp(2 * i + 1 + LEAD)
            if i == 1:
                half_copy(4, on_scalar, on_scalar)
                half_q(4)
                stage_act(0, whole)
            if i > 1:
                stage_act(i - 1, whole)
            if i > 1:
                half_q(2 * i + 2)
            if live(i - 3):
                stage_out(i - 3, whole)
            if live(i - 2):
                stage_sum(i - 2, whole)
            if i > 1:
                stage_gpsimd(i - 1)
            half_add(2 * i)
            half_add(2 * i + 1)
            if live(i - 2):
                stage_tanh_c(i - 2, whole)
            half_copy(2 * i + LEAD, on_scalar, on_scalar)
            half_copy(2 * i + LEAD + 1, on_scalar, on_scalar)
            half_q(2 * i + LEAD)
            if i == 1:
                stage_products_vector(0, whole)
            else:
                stage_ig_vector(i - 1)
        halves = [(0, TC // 2), (TC // 2, TC)]
        for js in halves:
            stage_act(last, js)
        stage_out(last - 2, whole)
        stage_sum(last - 1, whole)
        stage_tanh_c(last - 1, whole)
        for js in halves:
            stage_products_vector(last, js)
        stage_sum(last, halves[0])
        stage_tanh_c(last, halves[0])
        stage_out(last - 1, whole)
        stage_sum(last, halves[1])
        stage_tanh_c(last, halves[1])
        nc.sync.dma_start(out=out_2[0], in_=cn_tiles[last][:, TC - 1, :])
        for js in halves:
            stage_out(last, js)
        nc.scalar.dma_start(out=out_1[0], in_=hn_tiles[last][:, TC - 1, :])
